import numpy as np
import ml_dtypes


def mxq(x, axis, fmt="e4m3"):
    dtype, down = {"e4m3": (ml_dtypes.float8_e4m3fn, 7), "e5m2": (ml_dtypes.float8_e5m2, 14)}[fmt]
    v = np.moveaxis(np.asarray(x, np.float32).astype(ml_dtypes.bfloat16).astype(np.float64), axis, -1)
    blocks = v.reshape(v.shape[:-1] + (-1, 32))
    amax = np.abs(blocks).max(-1, keepdims=True)
    byte = np.maximum(np.where(amax > 0, np.frexp(amax)[1] - 1 + 127, 0) - down, 1)
    scale = np.exp2(byte - 127.0)
    codes = (blocks / scale).astype(np.float32).astype(dtype).astype(np.float64)
    return np.moveaxis((codes * scale).reshape(v.shape), -1, axis)


WIDE = False


def mx_kscale(k):
    if not WIDE:
        return np.ones(k)
    levels = np.array([10, -10, 5, -5, 0])
    a = np.random.permutation(np.resize(levels, k // 512 * 4)).reshape(k // 512, 4)
    idx = np.arange(k)
    return np.exp2(a[idx // 512, idx % 128 // 32])


BF16 = ml_dtypes.bfloat16


def bf(x):
    return np.asarray(x, np.float32).astype(BF16)


def f64(x):
    return np.asarray(x).astype(np.float64)


B, T, D, E, F = 4, 1024, 512, 1024, 256
EPS = 1e-6


def rms_norm(x, w):
    rms = np.sqrt(np.mean(x * x, axis=-1, keepdims=True) + EPS)
    return x / rms * w


def erf(v):
    a = np.minimum(np.abs(v), 6.0)
    z = 2.0 * a * a
    term = a.copy()
    tot = a.copy()
    for n in range(1, 110):
        term = term * z / (2 * n + 1)
        tot = tot + term
    return np.sign(v) * tot * np.exp(-a * a) * 2.0 / np.sqrt(np.pi)


def gelu_erf(v):
    return 0.5 * v * (1.0 + erf(v / np.sqrt(2.0)))


def setup_inputs():
    s, t = mx_kscale(E), mx_kscale(D)
    return {"attn": bf(np.random.standard_normal((B, T, E)) * 0.6 * s),
            "x": bf(np.random.standard_normal((B, T, D))),
            "wo": bf(np.random.standard_normal((E, D)) / np.sqrt(E) / s[:, None]),
            "bo": bf(np.random.standard_normal(D) * 0.1),
            "mlp_norm_w": bf((1.0 + 0.1 * np.random.standard_normal(D)) * t),
            "w1": bf(np.random.standard_normal((D, F)) / np.sqrt(D) / t[:, None]),
            "b1": bf(np.random.standard_normal(F) * 0.1)}


def reference(attn, x, wo, bo, mlp_norm_w, w1, b1):
    x_mid = f64(x) + (mxq(f64(attn), 2, "e4m3") @ mxq(f64(wo), 0, "e4m3")) + f64(bo)
    h = rms_norm(x_mid, f64(mlp_norm_w))
    g = gelu_erf((mxq(h, 2, "e4m3") @ mxq(f64(w1), 0, "e4m3")) + f64(b1))
    return x_mid, g

@@ -1,0 +1,277 @@
+from contextlib import ExitStack
+
+import concourse.mybir as mybir
+from concourse.masks import make_identity
+
+BF16 = mybir.dt.bfloat16
+F32 = mybir.dt.float32
+U32 = mybir.dt.uint32
+U8 = mybir.dt.uint8
+FP8X4 = mybir.dt.float8_e4m3fn_x4
+ALU = mybir.AluOpType
+ACT = mybir.ActivationFunctionType
+
+P = 128
+PACK = 4
+K_PASS = P * PACK
+PAIR = 2
+
+TOKENS, E, D, F = 4096, 1024, 512, 256
+EPS = 1e-6
+FLOPS = 2 * TOKENS * (E * D + D * F)
+
+E_PASSES = E // K_PASS
+F_CHUNKS = F // P
+TILES = 2
+UNIT = TILES * P
+UNITS = TOKENS // UNIT
+LOAD_AHEAD = 3
+
+
+def tile_tinyblock_pb_t_kernel(tc, attn, x, wo, bo, mlp_norm_w, w1, b1, out_0, out_1):
+    nc = tc.nc
+    attn_units = attn.flatten_outer_dims().rearrange("(u p j) k -> u p (j k)", p=P, j=TILES)
+    x_units = x.flatten_outer_dims().rearrange("(u p j) d -> u p j d", p=P, j=TILES)
+    x_mid_units = out_0.flatten_outer_dims().rearrange("(u p j) d -> u p j d", p=P, j=TILES)
+    g_units = out_1.flatten_outer_dims().rearrange("(u p j) f -> u p j f", p=P, j=TILES)
+
+    with ExitStack() as ctx:
+        const = ctx.enter_context(tc.tile_pool(name="const", bufs=1))
+        loads = ctx.enter_context(tc.tile_pool(name="loads", bufs=LOAD_AHEAD + 2))
+        pair = ctx.enter_context(tc.tile_pool(name="pair", bufs=2))
+        resid = ctx.enter_context(tc.tile_pool(name="resid", bufs=4))
+        ps_attn = ctx.enter_context(tc.psum_pool(name="ps_attn", bufs=TILES))
+        ps_prod = ctx.enter_context(tc.psum_pool(name="ps_prod", bufs=TILES + 1))
+        ps_one = ctx.enter_context(tc.psum_pool(name="ps_one", bufs=1))
+        ctx.enter_context(tc.manual_schedule())
+
+        attn_sb, x_sb, attn_grp, attn_codes, attn_scales = {}, {}, {}, {}, {}
+        attn_t, prod, x_mid, rstd, h_sb, h_t, h_grp = {}, {}, {}, {}, {}, {}, {}
+        h_codes, h_scales, pre_act, g_t, g_back = {}, {}, {}, {}, {}
+
+        def load_unit(u):
+            attn_sb[u] = loads.tile([P, TILES * E], BF16, name="attn_sb")
+            nc.sync.dma_start(out=attn_sb[u][:], in_=attn_units[u])
+            x_sb[u] = loads.tile([P, TILES, D], BF16, name="x_sb")
+            nc.sync.dma_start(out=x_sb[u][:], in_=x_units[u])
+
+        wo_raw = const.tile([P, E_PASSES, PACK, D], BF16, name="wo_raw")
+        for c in range(E_PASSES):
+            nc.sync.dma_start(
+                out=wo_raw[:, c].rearrange("p (h e) n -> p h (e n)", e=PAIR),
+                in_=wo[c * K_PASS : (c + 1) * K_PASS, :].rearrange("(h p e) n -> p h (e n)", p=P, e=PAIR),
+            )
+        for u in range(LOAD_AHEAD):
+            load_unit(u)
+
+        b1_rows = const.tile([P, P], BF16, name="b1_rows")
+        nc.vector.memset(b1_rows[:], 0.0)
+        nc.scalar.dma_start(out=b1_rows[0:F_CHUNKS, :], in_=b1.rearrange("(a f) -> a f", a=F_CHUNKS))
+        w1_raw = const.tile([P, PACK, F], BF16, name="w1_raw")
+        nc.scalar.dma_start(
+            out=w1_raw[:].rearrange("p (h e) n -> p h (e n)", e=PAIR),
+            in_=w1.rearrange("(h p e) n -> p h (e n)", p=P, e=PAIR),
+        )
+        bo_all = const.tile([P, D], BF16, name="bo_all")
+        nc.scalar.dma_start(out=bo_all[:], in_=bo.partition_broadcast(P))
+        gain_all = const.tile([P, D], BF16, name="gain_all")
+        nc.scalar.dma_start(out=gain_all[:], in_=mlp_norm_w.partition_broadcast(P))
+
+        ident = const.tile([P, P], F32, name="ident")
+        make_identity(nc, ident[:])
+        neg_half = const.tile([P, TILES], F32, name="neg_half")
+        nc.gpsimd.memset(neg_half[:], -0.5)
+
+        warm = const.tile([P, 1], F32, name="warm")
+        nc.vector.memset(warm[:], 0.0)
+        nc.scalar.activation(out=warm[:], in_=warm[:], func=ACT.Gelu)
+
+        b1_rows_f32 = const.tile([P, P], F32, name="b1_rows_f32")
+        nc.vector.tensor_copy(out=b1_rows_f32[:], in_=b1_rows[:])
+        b1_t = ps_one.tile([P, P], F32, name="g_back")
+        nc.tensor.transpose(b1_t[:], b1_rows_f32[:], ident[:])
+        b1_col = const.tile([P, F_CHUNKS], F32, name="b1_col")
+        nc.vector.tensor_copy(out=b1_col[:], in_=b1_t[:, 0:F_CHUNKS])
+
+        def group_weight(raw, grouped):
+            nc.vector.tensor_copy(
+                out=grouped.rearrange("p (n i) t -> p n t i", i=PACK),
+                in_=raw.rearrange("p t (n i) -> p n t i", i=PACK),
+            )
+
+        def quantise_weight(grouped, codes, scales):
+            nc.vector.quantize_mx(
+                out=codes.bitcast(FP8X4), scales=scales, in_=grouped.rearrange("p n t -> p (n t)")
+            )
+
+        wo_grp = const.tile([P, E_PASSES, D, PACK], BF16, name="wo_grp", align_bytes=64)
+        wo_codes = const.tile([P, E_PASSES, D], U32, name="wo_codes", align_bytes=64)
+        wo_scales = const.tile([P, E_PASSES, D], U8, name="wo_scales", align_bytes=64)
+        w1_grp = const.tile([P, F, PACK], BF16, name="w1_grp", align_bytes=64)
+        w1_codes = const.tile([P, F], U32, name="w1_codes", align_bytes=64)
+        w1_scales = const.tile([P, F], U8, name="w1_scales", align_bytes=64)
+        for c in range(E_PASSES):
+            group_weight(wo_raw[:, c], wo_grp[:, c])
+        group_weight(w1_raw[:], w1_grp[:])
+        for c in range(E_PASSES):
+            quantise_weight(wo_grp[:, c], wo_codes[:, c], wo_scales[:, c])
+        quantise_weight(w1_grp[:], w1_codes[:], w1_scales[:])
+
+        def transpose_attn(u):
+            words = attn_sb[u][:].bitcast(F32)
+            for j in range(TILES):
+                attn_t[u, j] = ps_attn.tile([P, E // PAIR // P, P], F32, name="attn_t")
+                for b in range(E // PAIR // P):
+                    first = j * (E // PAIR) + b * P
+                    nc.tensor.transpose(attn_t[u, j][:, b, :], words[:, first : first + P], ident[:])
+
+        def group_attn(u):
+            attn_grp[u] = pair.tile([P, TILES * E_PASSES * P * PACK], BF16, name="attn_grp", align_bytes=64)
+            words = attn_grp[u][:].bitcast(F32)
+            per_tile = E_PASSES * P * PAIR
+            for j in range(TILES):
+                nc.scalar.copy(
+                    out=words[:, j * per_tile : (j + 1) * per_tile].rearrange(
+                        "p (c r h) -> p c r h", c=E_PASSES, h=PAIR
+                    ),
+                    in_=attn_t[u, j][:].rearrange("p (c h) r -> p c r h", h=PAIR),
+                )
+
+        def quantise_attn(u):
+            attn_codes[u] = pair.tile([P, TILES * E_PASSES * P], U32, name="attn_codes", align_bytes=64)
+            attn_scales[u] = pair.tile([P, TILES * E_PASSES * P], U8, name="attn_scales", align_bytes=64)
+            nc.vector.quantize_mx(
+                out=attn_codes[u][:].bitcast(FP8X4), scales=attn_scales[u][:], in_=attn_grp[u][:]
+            )
+
+        def multiply_wo(u):
+            for j in range(TILES):
+                prod[u, j] = ps_prod.tile([P, D], F32, name="prod")
+                for c in range(E_PASSES):
+                    cols = slice((j * E_PASSES + c) * P, (j * E_PASSES + c + 1) * P)
+                    nc.tensor.matmul_mx(
+                        out=prod[u, j][:],
+                        lhsT=attn_codes[u][:, cols].bitcast(FP8X4),
+                        lhsT_scale=attn_scales[u][:, cols],
+                        rhs=wo_codes[:, c].bitcast(FP8X4),
+                        rhs_scale=wo_scales[:, c],
+                        start=(c == 0),
+                        stop=(c == E_PASSES - 1),
+                    )
+
+        def add_bias(u):
+            x_mid[u] = resid.tile([P, TILES, D], F32, name="x_mid")
+            nc.vector.tensor_tensor(
+                out=x_mid[u][:],
+                in0=x_sb[u][:],
+                in1=bo_all[:].unsqueeze(1).to_broadcast([P, TILES, D]),
+                op=ALU.add,
+            )
+
+        def add_product(u):
+            for j in range(TILES):
+                nc.vector.tensor_tensor(
+                    out=x_mid[u][:, j, :], in0=prod[u, j][:], in1=x_mid[u][:, j, :], op=ALU.add
+                )
+            nc.sync.dma_start(out=x_mid_units[u], in_=x_mid[u][:])
+
+        def inverse_rms(u):
+            sum_sq = resid.tile([P, TILES], F32, name="sum_sq")
+            for j in range(TILES):
+                squares = pair.tile([P, D], BF16, name="squares")
+                nc.scalar.activation(
+                    out=squares[:], in_=x_mid[u][:, j, :], func=ACT.Square, accum_out=sum_sq[:, j : j + 1]
+                )
+            mean_sq = resid.tile([P, TILES], F32, name="mean_sq")
+            nc.gpsimd.tensor_scalar(
+                out=mean_sq[:], in0=sum_sq[:], scalar1=1.0 / D, scalar2=EPS, op0=ALU.mult, op1=ALU.add
+            )
+            rstd[u] = resid.tile([P, TILES], F32, name="rstd")
+            nc.gpsimd.tensor_tensor(out=rstd[u][:], in0=mean_sq[:], in1=neg_half[:], op=ALU.pow)
+
+        def normalise(u):
+            h_sb[u] = pair.tile([P, TILES * D], BF16, name="h_sb")
+            for j in range(TILES):
+                nc.vector.scalar_tensor_tensor(
+                    out=h_sb[u][:, j * D : (j + 1) * D],
+                    in0=x_mid[u][:, j, :],
+                    scalar=rstd[u][:, j : j + 1],
+                    in1=gain_all[:],
+                    op0=ALU.mult,
+                    op1=ALU.mult,
+                )
+
+        def transpose_h(u):
+            words = h_sb[u][:].bitcast(F32)
+            h_t[u] = ps_one.tile([P, TILES, D // PAIR // P, P], F32, name="h_t")
+            for j in range(TILES):
+                for b in range(D // PAIR // P):
+                    first = j * (D // PAIR) + b * P
+                    nc.tensor.transpose(h_t[u][:, j, b, :], words[:, first : first + P], ident[:])
+
+        def group_h(u):
+            h_grp[u] = pair.tile([P, UNIT * PACK], BF16, name="h_grp", align_bytes=64)
+            nc.scalar.copy(
+                out=h_grp[u][:].bitcast(F32).rearrange("p (j r h) -> p j r h", j=TILES, h=PAIR),
+                in_=h_t[u][:].rearrange("p j h r -> p j r h"),
+            )
+
+        def quantise_h(u):
+            h_codes[u] = pair.tile([P, UNIT], U32, name="h_codes", align_bytes=64)
+            h_scales[u] = pair.tile([P, UNIT], U8, name="h_scales", align_bytes=64)
+            nc.vector.quantize_mx(out=h_codes[u][:].bitcast(FP8X4), scales=h_scales[u][:], in_=h_grp[u][:])
+
+        def multiply_w1(u):
+            pre_act[u] = ps_one.tile([P, F_CHUNKS, UNIT], F32, name="pre_act")
+            for a in range(F_CHUNKS):
+                nc.tensor.matmul_mx(
+                    out=pre_act[u][:, a, :],
+                    lhsT=w1_codes[:, a * P : (a + 1) * P].bitcast(FP8X4),
+                    lhsT_scale=w1_scales[:, a * P : (a + 1) * P],
+                    rhs=h_codes[u][:].bitcast(FP8X4),
+                    rhs_scale=h_scales[u][:],
+                    start=True,
+                    stop=True,
+                )
+
+        def gelu(u):
+            g_t[u] = pair.tile([P, F_CHUNKS, UNIT], F32, name="g_t")
+            for a in range(F_CHUNKS):
+                nc.scalar.activation(
+                    out=g_t[u][:, a, :], in_=pre_act[u][:, a, :], func=ACT.Gelu, bias=b1_col[:, a : a + 1]
+                )
+
+        def transpose_g(u):
+            g_back[u] = ps_one.tile([P, TILES, F], F32, name="g_back")
+            for j in range(TILES):
+                for a in range(F_CHUNKS):
+                    nc.tensor.transpose(
+                        g_back[u][:, j, a * P : (a + 1) * P], g_t[u][:, a, j * P : (j + 1) * P], ident[:]
+                    )
+
+        def store_g(u):
+            g_sb = resid.tile([P, TILES, F], F32, name="g_sb")
+            nc.scalar.copy(out=g_sb[:], in_=g_back[u][:])
+            nc.sync.dma_start(out=g_units[u], in_=g_sb[:])
+
+        def run(stage, u):
+            if 0 <= u < UNITS:
+                stage(u)
+
+        for n in range(-1, UNITS + 6):
+            run(load_unit, n + LOAD_AHEAD + 1)
+            run(transpose_h, n - 3)
+            run(transpose_g, n - 6)
+            run(transpose_attn, n + 1)
+            run(quantise_attn, n)
+            run(gelu, n - 5)
+            run(multiply_wo, n)
+            run(multiply_w1, n - 4)
+            run(group_h, n - 3)
+            run(store_g, n - 6)
+            run(add_product, n - 1)
+            run(group_attn, n + 1)
+            run(add_bias, n)
+            run(inverse_rms, n - 1)
+            run(normalise, n - 2)
+            run(quantise_h, n - 3)

@@ -55,43 +55,57 @@ def tile_tinyblock_pb_t_kernel(tc, attn, x, wo, bo, mlp_norm_w, w1, b1, out_0, o
             x_sb[u] = loads.tile([P, TILES, D], BF16, name="x_sb")
             nc.sync.dma_start(out=x_sb[u][:], in_=x_units[u])
 
-        wo_raw = const.tile([P, E_PASSES, PACK, D], BF16, name="wo_raw")
-        for c in range(E_PASSES):
-            nc.sync.dma_start(
-                out=wo_raw[:, c].rearrange("p (h e) n -> p h (e n)", e=PAIR),
-                in_=wo[c * K_PASS : (c + 1) * K_PASS, :].rearrange("(h p e) n -> p h (e n)", p=P, e=PAIR),
-            )
-        for u in range(LOAD_AHEAD):
-            load_unit(u)
-
+        ones = const.tile([P, P], BF16, name="ones")
+        nc.vector.memset(ones[:], 1.0)
+        bo_row = const.tile([P, D], BF16, name="bo_row")
+        nc.vector.memset(bo_row[:], 0.0)
+        gain_row = const.tile([P, D], BF16, name="gain_row")
+        nc.vector.memset(gain_row[:], 0.0)
         b1_rows = const.tile([P, P], BF16, name="b1_rows")
         nc.vector.memset(b1_rows[:], 0.0)
+        warm = const.tile([P, 1], F32, name="warm")
+        nc.vector.memset(warm[:], 0.0)
+        nc.scalar.dma_start(out=bo_row[0:1, :], in_=bo.rearrange("(o d) -> o d", o=1))
+        nc.scalar.dma_start(out=gain_row[0:1, :], in_=mlp_norm_w.rearrange("(o d) -> o d", o=1))
         nc.scalar.dma_start(out=b1_rows[0:F_CHUNKS, :], in_=b1.rearrange("(a f) -> a f", a=F_CHUNKS))
         w1_raw = const.tile([P, PACK, F], BF16, name="w1_raw")
         nc.scalar.dma_start(
             out=w1_raw[:].rearrange("p (h e) n -> p h (e n)", e=PAIR),
             in_=w1.rearrange("(h p e) n -> p h (e n)", p=P, e=PAIR),
         )
-        bo_all = const.tile([P, D], BF16, name="bo_all")
-        nc.scalar.dma_start(out=bo_all[:], in_=bo.partition_broadcast(P))
-        gain_all = const.tile([P, D], BF16, name="gain_all")
-        nc.scalar.dma_start(out=gain_all[:], in_=mlp_norm_w.partition_broadcast(P))
+
+        wo_raw = const.tile([P, E_PASSES, PACK, D], BF16, name="wo_raw")
+        for c in range(E_PASSES):
+            nc.sync.dma_start(
+                out=wo_raw[:, c].rearrange("p (h e) n -> p h (e n)", e=PAIR),
+                in_=wo[c * K_PASS : (c + 1) * K_PASS, :].rearrange("(h p e) n -> p h (e n)", p=P, e=PAIR),
+            )
+        for u in range(LOAD_AHEAD + 1):
+            load_unit(u)
 
         ident = const.tile([P, P], F32, name="ident")
         make_identity(nc, ident[:])
         neg_half = const.tile([P, TILES], F32, name="neg_half")
         nc.gpsimd.memset(neg_half[:], -0.5)
 
-        warm = const.tile([P, 1], F32, name="warm")
-        nc.vector.memset(warm[:], 0.0)
         nc.scalar.activation(out=warm[:], in_=warm[:], func=ACT.Gelu)
 
+        def on_every_partition(row, name):
+            summed = ps_prod.tile([P, D], F32, name="prod")
+            nc.tensor.matmul(summed[:], lhsT=ones[:], rhs=row[:], start=True, stop=True)
+            spread = const.tile([P, D], BF16, name=name)
+            nc.scalar.copy(out=spread[:], in_=summed[:])
+            return spread
+
+        bo_all = on_every_partition(bo_row, "bo_all")
+        gain_all = on_every_partition(gain_row, "gain_all")
+
         b1_rows_f32 = const.tile([P, P], F32, name="b1_rows_f32")
-        nc.vector.tensor_copy(out=b1_rows_f32[:], in_=b1_rows[:])
+        nc.scalar.copy(out=b1_rows_f32[:], in_=b1_rows[:])
         b1_t = ps_one.tile([P, P], F32, name="g_back")
         nc.tensor.transpose(b1_t[:], b1_rows_f32[:], ident[:])
         b1_col = const.tile([P, F_CHUNKS], F32, name="b1_col")
-        nc.vector.tensor_copy(out=b1_col[:], in_=b1_t[:, 0:F_CHUNKS])
+        nc.scalar.copy(out=b1_col[:], in_=b1_t[:, 0:F_CHUNKS])
 
         def group_weight(raw, grouped):
             nc.vector.tensor_copy(
@@ -110,12 +124,6 @@ def tile_tinyblock_pb_t_kernel(tc, attn, x, wo, bo, mlp_norm_w, w1, b1, out_0, o
         w1_grp = const.tile([P, F, PACK], BF16, name="w1_grp", align_bytes=64)
         w1_codes = const.tile([P, F], U32, name="w1_codes", align_bytes=64)
         w1_scales = const.tile([P, F], U8, name="w1_scales", align_bytes=64)
-        for c in range(E_PASSES):
-            group_weight(wo_raw[:, c], wo_grp[:, c])
-        group_weight(w1_raw[:], w1_grp[:])
-        for c in range(E_PASSES):
-            quantise_weight(wo_grp[:, c], wo_codes[:, c], wo_scales[:, c])
-        quantise_weight(w1_grp[:], w1_codes[:], w1_scales[:])
 
         def transpose_attn(u):
             words = attn_sb[u][:].bitcast(F32)
@@ -258,20 +266,29 @@ def tile_tinyblock_pb_t_kernel(tc, attn, x, wo, bo, mlp_norm_w, w1, b1, out_0, o
             if 0 <= u < UNITS:
                 stage(u)
 
-        for n in range(-1, UNITS + 6):
+        transpose_attn(0)
+        group_attn(0)
+        for c in range(E_PASSES):
+            group_weight(wo_raw[:, c], wo_grp[:, c])
+        group_weight(w1_raw[:], w1_grp[:])
+        for c in range(E_PASSES):
+            quantise_weight(wo_grp[:, c], wo_codes[:, c], wo_scales[:, c])
+        quantise_weight(w1_grp[:], w1_codes[:], w1_scales[:])
+
+        for n in range(UNITS + 4):
             run(load_unit, n + LOAD_AHEAD + 1)
             run(transpose_h, n - 3)
-            run(transpose_g, n - 6)
             run(transpose_attn, n + 1)
+            run(transpose_g, n - 4)
             run(quantise_attn, n)
-            run(gelu, n - 5)
-            run(multiply_wo, n)
-            run(multiply_w1, n - 4)
             run(group_h, n - 3)
-            run(store_g, n - 6)
+            run(multiply_wo, n)
             run(add_product, n - 1)
             run(group_attn, n + 1)
+            run(quantise_h, n - 3)
+            run(multiply_w1, n - 3)
+            run(store_g, n - 4)
             run(add_bias, n)
             run(inverse_rms, n - 1)
+            run(gelu, n - 3)
             run(normalise, n - 2)
-            run(quantise_h, n - 3)

@@ -41,7 +41,7 @@ def tile_tinyblock_pb_t_kernel(tc, attn, x, wo, bo, mlp_norm_w, w1, b1, out_0, o
         pair = ctx.enter_context(tc.tile_pool(name="pair", bufs=2))
         resid = ctx.enter_context(tc.tile_pool(name="resid", bufs=4))
         ps_attn = ctx.enter_context(tc.psum_pool(name="ps_attn", bufs=TILES))
-        ps_prod = ctx.enter_context(tc.psum_pool(name="ps_prod", bufs=TILES + 1))
+        ps_prod = ctx.enter_context(tc.psum_pool(name="ps_prod", bufs=TILES))
         ps_one = ctx.enter_context(tc.psum_pool(name="ps_one", bufs=1))
         ctx.enter_context(tc.manual_schedule())
 
@@ -90,15 +90,11 @@ def tile_tinyblock_pb_t_kernel(tc, attn, x, wo, bo, mlp_norm_w, w1, b1, out_0, o
 
         nc.scalar.activation(out=warm[:], in_=warm[:], func=ACT.Gelu)
 
-        def on_every_partition(row, name):
-            summed = ps_prod.tile([P, D], F32, name="prod")
-            nc.tensor.matmul(summed[:], lhsT=ones[:], rhs=row[:], start=True, stop=True)
-            spread = const.tile([P, D], BF16, name=name)
-            nc.scalar.copy(out=spread[:], in_=summed[:])
-            return spread
-
-        bo_all = on_every_partition(bo_row, "bo_all")
-        gain_all = on_every_partition(gain_row, "gain_all")
+        spread = ps_one.tile([P, 2, D], BF16, name="spread")
+        nc.tensor.matmul(spread[:, 0, :], lhsT=ones[:], rhs=bo_row[:], start=True, stop=True)
+        nc.tensor.matmul(spread[:, 1, :], lhsT=ones[:], rhs=gain_row[:], start=True, stop=True)
+        bo_all = spread[:, 0, :]
+        gain_all = spread[:, 1, :]
 
         b1_rows_f32 = const.tile([P, P], F32, name="b1_rows_f32")
         nc.scalar.copy(out=b1_rows_f32[:], in_=b1_rows[:])
@@ -172,7 +168,7 @@ def tile_tinyblock_pb_t_kernel(tc, attn, x, wo, bo, mlp_norm_w, w1, b1, out_0, o
             nc.vector.tensor_tensor(
                 out=x_mid[u][:],
                 in0=x_sb[u][:],
-                in1=bo_all[:].unsqueeze(1).to_broadcast([P, TILES, D]),
+                in1=bo_all.unsqueeze(1).to_broadcast([P, TILES, D]),
                 op=ALU.add,
             )
 
@@ -204,7 +200,7 @@ def tile_tinyblock_pb_t_kernel(tc, attn, x, wo, bo, mlp_norm_w, w1, b1, out_0, o
                     out=h_sb[u][:, j * D : (j + 1) * D],
                     in0=x_mid[u][:, j, :],
                     scalar=rstd[u][:, j : j + 1],
-                    in1=gain_all[:],
+                    in1=gain_all,
                     op0=ALU.mult,
                     op1=ALU.mult,
                 )

@@ -187,9 +187,7 @@ def tile_tinyblock_pb_t_kernel(tc, attn, x, wo, bo, mlp_norm_w, w1, b1, out_0, o
                     out=squares[:], in_=x_mid[u][:, j, :], func=ACT.Square, accum_out=sum_sq[:, j : j + 1]
                 )
             mean_sq = resid.tile([P, TILES], F32, name="mean_sq")
-            nc.gpsimd.tensor_scalar(
-                out=mean_sq[:], in0=sum_sq[:], scalar1=1.0 / D, scalar2=EPS, op0=ALU.mult, op1=ALU.add
-            )
+            nc.scalar.activation(out=mean_sq[:], in_=sum_sq[:], func=ACT.Copy, scale=1.0 / D, bias=EPS)
             rstd[u] = resid.tile([P, TILES], F32, name="rstd")
             nc.gpsimd.tensor_tensor(out=rstd[u][:], in0=mean_sq[:], in1=neg_half[:], op=ALU.pow)
 

from contextlib import ExitStack

import concourse.mybir as mybir
from concourse.masks import make_identity

BF16 = mybir.dt.bfloat16
F32 = mybir.dt.float32
U32 = mybir.dt.uint32
U8 = mybir.dt.uint8
FP8X4 = mybir.dt.float8_e4m3fn_x4
ALU = mybir.AluOpType
ACT = mybir.ActivationFunctionType

P = 128
PACK = 4
K_PASS = P * PACK
PAIR = 2

TOKENS, E, D, F = 4096, 1024, 512, 256
EPS = 1e-6
FLOPS = 2 * TOKENS * (E * D + D * F)

E_PASSES = E // K_PASS
F_CHUNKS = F // P
TILES = 2
UNIT = TILES * P
UNITS = TOKENS // UNIT
LOAD_AHEAD = 3


def tile_tinyblock_pb_t_kernel(tc, attn, x, wo, bo, mlp_norm_w, w1, b1, out_0, out_1):
    nc = tc.nc
    attn_units = attn.flatten_outer_dims().rearrange("(u p j) k -> u p (j k)", p=P, j=TILES)
    x_units = x.flatten_outer_dims().rearrange("(u p j) d -> u p j d", p=P, j=TILES)
    x_mid_units = out_0.flatten_outer_dims().rearrange("(u p j) d -> u p j d", p=P, j=TILES)
    g_units = out_1.flatten_outer_dims().rearrange("(u p j) f -> u p j f", p=P, j=TILES)

    with ExitStack() as ctx:
        const = ctx.enter_context(tc.tile_pool(name="const", bufs=1))
        loads = ctx.enter_context(tc.tile_pool(name="loads", bufs=LOAD_AHEAD + 2))
        pair = ctx.enter_context(tc.tile_pool(name="pair", bufs=2))
        resid = ctx.enter_context(tc.tile_pool(name="resid", bufs=4))
        ps_attn = ctx.enter_context(tc.psum_pool(name="ps_attn", bufs=TILES))
        ps_prod = ctx.enter_context(tc.psum_pool(name="ps_prod", bufs=TILES))
        ps_one = ctx.enter_context(tc.psum_pool(name="ps_one", bufs=1))
        ctx.enter_context(tc.manual_schedule())

        attn_sb, x_sb, attn_grp, attn_codes, attn_scales = {}, {}, {}, {}, {}
        attn_t, prod, x_mid, rstd, h_sb, h_t, h_grp = {}, {}, {}, {}, {}, {}, {}
        h_codes, h_scales, pre_act, g_t, g_back = {}, {}, {}, {}, {}

        def load_unit(u):
            attn_sb[u] = loads.tile([P, TILES * E], BF16, name="attn_sb")
            nc.sync.dma_start(out=attn_sb[u][:], in_=attn_units[u])
            x_sb[u] = loads.tile([P, TILES, D], BF16, name="x_sb")
            nc.sync.dma_start(out=x_sb[u][:], in_=x_units[u])

        ones = const.tile([P, P], BF16, name="ones")
        nc.vector.memset(ones[:], 1.0)
        bo_row = const.tile([P, D], BF16, name="bo_row")
        nc.vector.memset(bo_row[:], 0.0)
        gain_row = const.tile([P, D], BF16, name="gain_row")
        nc.vector.memset(gain_row[:], 0.0)
        b1_rows = const.tile([P, P], BF16, name="b1_rows")
        nc.vector.memset(b1_rows[:], 0.0)
        warm = const.tile([P, 1], F32, name="warm")
        nc.vector.memset(warm[:], 0.0)
        nc.scalar.dma_start(out=bo_row[0:1, :], in_=bo.rearrange("(o d) -> o d", o=1))
        nc.scalar.dma_start(out=gain_row[0:1, :], in_=mlp_norm_w.rearrange("(o d) -> o d", o=1))
        nc.scalar.dma_start(out=b1_rows[0:F_CHUNKS, :], in_=b1.rearrange("(a f) -> a f", a=F_CHUNKS))
        w1_raw = const.tile([P, PACK, F], BF16, name="w1_raw")
        nc.scalar.dma_start(
            out=w1_raw[:].rearrange("p (h e) n -> p h (e n)", e=PAIR),
            in_=w1.rearrange("(h p e) n -> p h (e n)", p=P, e=PAIR),
        )

        wo_raw = const.tile([P, E_PASSES, PACK, D], BF16, name="wo_raw")
        for c in range(E_PASSES):
            nc.sync.dma_start(
                out=wo_raw[:, c].rearrange("p (h e) n -> p h (e n)", e=PAIR),
                in_=wo[c * K_PASS : (c + 1) * K_PASS, :].rearrange("(h p e) n -> p h (e n)", p=P, e=PAIR),
            )
        for u in range(LOAD_AHEAD + 1):
            load_unit(u)

        ident = const.tile([P, P], F32, name="ident")
        make_identity(nc, ident[:])
        neg_half = const.tile([P, TILES], F32, name="neg_half")
        nc.gpsimd.memset(neg_half[:], -0.5)

        nc.scalar.activation(out=warm[:], in_=warm[:], func=ACT.Gelu)

        spread = ps_one.tile([P, 2, D], BF16, name="spread")
        nc.tensor.matmul(spread[:, 0, :], lhsT=ones[:], rhs=bo_row[:], start=True, stop=True)
        nc.tensor.matmul(spread[:, 1, :], lhsT=ones[:], rhs=gain_row[:], start=True, stop=True)
        bo_all = spread[:, 0, :]
        gain_all = spread[:, 1, :]

        b1_rows_f32 = const.tile([P, P], F32, name="b1_rows_f32")
        nc.scalar.copy(out=b1_rows_f32[:], in_=b1_rows[:])
        b1_t = ps_one.tile([P, P], F32, name="g_back")
        nc.tensor.transpose(b1_t[:], b1_rows_f32[:], ident[:])
        b1_col = const.tile([P, F_CHUNKS], F32, name="b1_col")
        nc.scalar.copy(out=b1_col[:], in_=b1_t[:, 0:F_CHUNKS])

        def group_weight(raw, grouped):
            nc.vector.tensor_copy(
                out=grouped.rearrange("p (n i) t -> p n t i", i=PACK),
                in_=raw.rearrange("p t (n i) -> p n t i", i=PACK),
            )

        def quantise_weight(grouped, codes, scales):
            nc.vector.quantize_mx(
                out=codes.bitcast(FP8X4), scales=scales, in_=grouped.rearrange("p n t -> p (n t)")
            )

        wo_grp = const.tile([P, E_PASSES, D, PACK], BF16, name="wo_grp", align_bytes=64)
        wo_codes = const.tile([P, E_PASSES, D], U32, name="wo_codes", align_bytes=64)
        wo_scales = const.tile([P, E_PASSES, D], U8, name="wo_scales", align_bytes=64)
        w1_grp = const.tile([P, F, PACK], BF16, name="w1_grp", align_bytes=64)
        w1_codes = const.tile([P, F], U32, name="w1_codes", align_bytes=64)
        w1_scales = const.tile([P, F], U8, name="w1_scales", align_bytes=64)

        def transpose_attn(u):
            words = attn_sb[u][:].bitcast(F32)
            for j in range(TILES):
                attn_t[u, j] = ps_attn.tile([P, E // PAIR // P, P], F32, name="attn_t")
                for b in range(E // PAIR // P):
                    first = j * (E // PAIR) + b * P
                    nc.tensor.transpose(attn_t[u, j][:, b, :], words[:, first : first + P], ident[:])

        def group_attn(u):
            attn_grp[u] = pair.tile([P, TILES * E_PASSES * P * PACK], BF16, name="attn_grp", align_bytes=64)
            words = attn_grp[u][:].bitcast(F32)
            per_tile = E_PASSES * P * PAIR
            for j in range(TILES):
                nc.scalar.copy(
                    out=words[:, j * per_tile : (j + 1) * per_tile].rearrange(
                        "p (c r h) -> p c r h", c=E_PASSES, h=PAIR
                    ),
                    in_=attn_t[u, j][:].rearrange("p (c h) r -> p c r h", h=PAIR),
                )

        def quantise_attn(u):
            attn_codes[u] = pair.tile([P, TILES * E_PASSES * P], U32, name="attn_codes", align_bytes=64)
            attn_scales[u] = pair.tile([P, TILES * E_PASSES * P], U8, name="attn_scales", align_bytes=64)
            nc.vector.quantize_mx(
                out=attn_codes[u][:].bitcast(FP8X4), scales=attn_scales[u][:], in_=attn_grp[u][:]
            )

        def multiply_wo(u):
            for j in range(TILES):
                prod[u, j] = ps_prod.tile([P, D], F32, name="prod")
                for c in range(E_PASSES):
                    cols = slice((j * E_PASSES + c) * P, (j * E_PASSES + c + 1) * P)
                    nc.tensor.matmul_mx(
                        out=prod[u, j][:],
                        lhsT=attn_codes[u][:, cols].bitcast(FP8X4),
                        lhsT_scale=attn_scales[u][:, cols],
                        rhs=wo_codes[:, c].bitcast(FP8X4),
                        rhs_scale=wo_scales[:, c],
                        start=(c == 0),
                        stop=(c == E_PASSES - 1),
                    )

        def add_bias(u):
            x_mid[u] = resid.tile([P, TILES, D], F32, name="x_mid")
            nc.vector.tensor_tensor(
                out=x_mid[u][:],
                in0=x_sb[u][:],
                in1=bo_all.unsqueeze(1).to_broadcast([P, TILES, D]),
                op=ALU.add,
            )

        def add_product(u):
            for j in range(TILES):
                nc.vector.tensor_tensor(
                    out=x_mid[u][:, j, :], in0=prod[u, j][:], in1=x_mid[u][:, j, :], op=ALU.add
                )
            nc.sync.dma_start(out=x_mid_units[u], in_=x_mid[u][:])

        def inverse_rms(u):
            sum_sq = resid.tile([P, TILES], F32, name="sum_sq")
            for j in range(TILES):
                squares = pair.tile([P, D], BF16, name="squares")
                nc.scalar.activation(
                    out=squares[:], in_=x_mid[u][:, j, :], func=ACT.Square, accum_out=sum_sq[:, j : j + 1]
                )
            mean_sq = resid.tile([P, TILES], F32, name="mean_sq")
            nc.scalar.activation(out=mean_sq[:], in_=sum_sq[:], func=ACT.Copy, scale=1.0 / D, bias=EPS)
            rstd[u] = resid.tile([P, TILES], F32, name="rstd")
            nc.gpsimd.tensor_tensor(out=rstd[u][:], in0=mean_sq[:], in1=neg_half[:], op=ALU.pow)

        def normalise(u):
            h_sb[u] = pair.tile([P, TILES * D], BF16, name="h_sb")
            for j in range(TILES):
                nc.vector.scalar_tensor_tensor(
                    out=h_sb[u][:, j * D : (j + 1) * D],
                    in0=x_mid[u][:, j, :],
                    scalar=rstd[u][:, j : j + 1],
                    in1=gain_all,
                    op0=ALU.mult,
                    op1=ALU.mult,
                )

        def transpose_h(u):
            words = h_sb[u][:].bitcast(F32)
            h_t[u] = ps_one.tile([P, TILES, D // PAIR // P, P], F32, name="h_t")
            for j in range(TILES):
                for b in range(D // PAIR // P):
                    first = j * (D // PAIR) + b * P
                    nc.tensor.transpose(h_t[u][:, j, b, :], words[:, first : first + P], ident[:])

        def group_h(u):
            h_grp[u] = pair.tile([P, UNIT * PACK], BF16, name="h_grp", align_bytes=64)
            nc.scalar.copy(
                out=h_grp[u][:].bitcast(F32).rearrange("p (j r h) -> p j r h", j=TILES, h=PAIR),
                in_=h_t[u][:].rearrange("p j h r -> p j r h"),
            )

        def quantise_h(u):
            h_codes[u] = pair.tile([P, UNIT], U32, name="h_codes", align_bytes=64)
            h_scales[u] = pair.tile([P, UNIT], U8, name="h_scales", align_bytes=64)
            nc.vector.quantize_mx(out=h_codes[u][:].bitcast(FP8X4), scales=h_scales[u][:], in_=h_grp[u][:])

        def multiply_w1(u):
            pre_act[u] = ps_one.tile([P, F_CHUNKS, UNIT], F32, name="pre_act")
            for a in range(F_CHUNKS):
                nc.tensor.matmul_mx(
                    out=pre_act[u][:, a, :],
                    lhsT=w1_codes[:, a * P : (a + 1) * P].bitcast(FP8X4),
                    lhsT_scale=w1_scales[:, a * P : (a + 1) * P],
                    rhs=h_codes[u][:].bitcast(FP8X4),
                    rhs_scale=h_scales[u][:],
                    start=True,
                    stop=True,
                )

        def gelu(u):
            g_t[u] = pair.tile([P, F_CHUNKS, UNIT], F32, name="g_t")
            for a in range(F_CHUNKS):
                nc.scalar.activation(
                    out=g_t[u][:, a, :], in_=pre_act[u][:, a, :], func=ACT.Gelu, bias=b1_col[:, a : a + 1]
                )

        def transpose_g(u):
            g_back[u] = ps_one.tile([P, TILES, F], F32, name="g_back")
            for j in range(TILES):
                for a in range(F_CHUNKS):
                    nc.tensor.transpose(
                        g_back[u][:, j, a * P : (a + 1) * P], g_t[u][:, a, j * P : (j + 1) * P], ident[:]
                    )

        def store_g(u):
            g_sb = resid.tile([P, TILES, F], F32, name="g_sb")
            nc.scalar.copy(out=g_sb[:], in_=g_back[u][:])
            nc.sync.dma_start(out=g_units[u], in_=g_sb[:])

        def run(stage, u):
            if 0 <= u < UNITS:
                stage(u)

        transpose_attn(0)
        group_attn(0)
        for c in range(E_PASSES):
            group_weight(wo_raw[:, c], wo_grp[:, c])
        group_weight(w1_raw[:], w1_grp[:])
        for c in range(E_PASSES):
            quantise_weight(wo_grp[:, c], wo_codes[:, c], wo_scales[:, c])
        quantise_weight(w1_grp[:], w1_codes[:], w1_scales[:])

        for n in range(UNITS + 4):
            run(load_unit, n + LOAD_AHEAD + 1)
            run(transpose_h, n - 3)
            run(transpose_attn, n + 1)
            run(transpose_g, n - 4)
            run(quantise_attn, n)
            run(group_h, n - 3)
            run(multiply_wo, n)
            run(add_product, n - 1)
            run(group_attn, n + 1)
            run(quantise_h, n - 3)
            run(multiply_w1, n - 3)
            run(store_g, n - 4)
            run(add_bias, n)
            run(inverse_rms, n - 1)
            run(gelu, n - 3)
            run(normalise, n - 2)
